import numpy as np
import ml_dtypes


def mxq(x, axis, fmt="e4m3"):
    dtype, down = {"e4m3": (ml_dtypes.float8_e4m3fn, 7), "e5m2": (ml_dtypes.float8_e5m2, 14)}[fmt]
    v = np.moveaxis(np.asarray(x, np.float32).astype(ml_dtypes.bfloat16).astype(np.float64), axis, -1)
    blocks = v.reshape(v.shape[:-1] + (-1, 32))
    amax = np.abs(blocks).max(-1, keepdims=True)
    byte = np.maximum(np.where(amax > 0, np.frexp(amax)[1] - 1 + 127, 0) - down, 1)
    scale = np.exp2(byte - 127.0)
    codes = (blocks / scale).astype(np.float32).astype(dtype).astype(np.float64)
    return np.moveaxis((codes * scale).reshape(v.shape), -1, axis)


WIDE = False


def mx_kscale(k):
    if not WIDE:
        return np.ones(k)
    levels = np.array([20, -20, 10, -10, 0])
    a = np.random.permutation(np.resize(levels, k // 512 * 4)).reshape(k // 512, 4)
    idx = np.arange(k)
    return np.exp2(a[idx // 512, idx % 128 // 32])


BF16 = ml_dtypes.bfloat16


def bf(x):
    return np.asarray(x, np.float32).astype(BF16)


def f64(x):
    return np.asarray(x).astype(np.float64)


B, F, G, N, L = 512, 512, 512, 100, 2
S2 = (L + 1) ** 2
C = sum((2 * l + 1) ** 2 for l in range(L + 1))


def setup_inputs():
    k = mx_kscale(B)
    x = np.random.standard_normal((B, F, S2)) * k[:, None, None]
    psi = np.random.standard_normal((G, F, S2))
    g = np.random.standard_normal((G, B, C)) * np.exp2(np.random.randint(-12, 1, (1, B, 1))) * 4.0 / k[None, :, None]
    return {"x": bf(x), "psi": bf(psi), "grad_out": bf(g)}


def reference(x, psi, grad_out):
    xq = mxq(f64(x), 0, "e4m3")
    gq = mxq(f64(grad_out), 1, "e5m2")
    scale = 1.0 / np.sqrt(F)
    outs = []
    c = 0
    for l in range(L + 1):
        s, d = l * l, 2 * l + 1
        a = xq[:, :, s:s + d].transpose(1, 2, 0).reshape(F, d * B)
        p = gq[:, :, c:c + d * d].reshape(G, B, d, d).transpose(2, 1, 0, 3).reshape(d * B, G * d)
        o = scale * (a @ p)
        outs.append(o.reshape(F, G, d).transpose(1, 0, 2))
        c += d * d
    return np.concatenate(outs, axis=-1)

@@ -1,0 +1,156 @@
+import math
+from contextlib import ExitStack
+
+import concourse.mybir as mybir
+
+BF16 = mybir.dt.bfloat16
+F32 = mybir.dt.float32
+U32 = mybir.dt.uint32
+U8 = mybir.dt.uint8
+E4M3_X4 = mybir.dt.float8_e4m3fn_x4
+E5M2_X4 = mybir.dt.float8_e5m2_x4
+
+P = 128
+PACK = 4
+BATCH = P * PACK
+F_IN = 512
+G_OUT = 512
+DEGREES = 3
+COEFFS = DEGREES * DEGREES
+POSITIONS = sum((2 * l + 1) ** 2 for l in range(DEGREES))
+G_TILE = P
+N_G_TILES = G_OUT // G_TILE
+SCALE = 1.0 / math.sqrt(F_IN)
+
+RUN = 4
+RECORD = PACK * POSITIONS
+RECORD_PITCH = 144
+F_PIECE = 128
+F_HALF = 256
+
+FLOPS = 2 * BATCH * F_IN * G_OUT * POSITIONS
+BYTES = 2 * BATCH * F_IN * COEFFS + 2 * G_OUT * BATCH * POSITIONS + 4 * G_OUT * F_IN * COEFFS
+
+
+def power_of_two_runs(total):
+    runs = []
+    start = 0
+    length = RUN
+    while start < total:
+        while start + length > total:
+            length //= 2
+        runs.append((start, length))
+        start += length
+    return runs
+
+
+def regroup(nc, turn, out, in_):
+    if turn % 2 == 0:
+        nc.vector.tensor_copy(out=out, in_=in_)
+    else:
+        nc.scalar.copy(out=out, in_=in_)
+
+
+def quantise_x(tc, x, x_words, x_scales):
+    nc = tc.nc
+    with tc.tile_pool(name="x_stage", bufs=1) as stage:
+        x_raw = stage.tile([P, PACK, F_IN, COEFFS], BF16)
+        x_rows = x.rearrange("(p j) f i -> p j f i", j=PACK)
+        for f0 in range(0, F_IN, F_PIECE):
+            piece = slice(f0, f0 + F_PIECE)
+            nc.sync.dma_start(out=x_raw[:, :, piece, :], in_=x_rows[:, :, piece, :])
+
+        x_grouped = stage.tile([P, COEFFS, F_IN, PACK], BF16, align_bytes=64)
+        turn = 0
+        for f0 in range(0, F_IN, F_PIECE):
+            piece = slice(f0, f0 + F_PIECE)
+            for i0, n in power_of_two_runs(COEFFS):
+                regroup(
+                    nc,
+                    turn,
+                    out=x_grouped[:, i0 : i0 + n, piece, :].rearrange("p i f j -> p f j i"),
+                    in_=x_raw[:, :, piece, i0 : i0 + n].rearrange("p j f i -> p f j i"),
+                )
+                turn += 1
+
+        for i in range(COEFFS):
+            nc.vector.quantize_mx(
+                out=x_words[:, i, :].bitcast(E4M3_X4),
+                scales=x_scales[:, i, :],
+                in_=x_grouped[:, i, :, :].rearrange("p f j -> p (f j)"),
+            )
+
+
+def tile_s2conv_pa_kernel(tc, x, psi, grad_out, out):
+    nc = tc.nc
+    with ExitStack() as pools:
+        keep = pools.enter_context(tc.tile_pool(name="keep", bufs=1))
+        raw_pool = pools.enter_context(tc.tile_pool(name="grad_raw", bufs=3))
+
+        x_words = keep.tile([P, COEFFS, F_IN], U32, align_bytes=64)
+        x_scales = keep.tile([P, COEFFS, F_IN], U8, align_bytes=64)
+        quantise_x(tc, x, x_words, x_scales)
+
+        grouped_pool = pools.enter_context(tc.tile_pool(name="grad_grouped", bufs=4))
+        words_pool = pools.enter_context(tc.tile_pool(name="grad_words", bufs=2))
+        planes_pool = pools.enter_context(tc.tile_pool(name="planes", bufs=1))
+        result_pool = pools.enter_context(tc.tile_pool(name="result", bufs=2))
+        psum = pools.enter_context(tc.psum_pool(name="psum", bufs=8))
+
+        turn = 0
+        for g0 in range(0, G_OUT, G_TILE):
+            g_raw = raw_pool.tile([P, G_TILE, RECORD_PITCH], BF16)
+            for h0 in range(0, G_TILE, G_TILE // 2):
+                nc.sync.dma_start(
+                    out=g_raw[:, h0 : h0 + G_TILE // 2, 0:RECORD],
+                    in_=grad_out[g0 + h0 : g0 + h0 + G_TILE // 2].rearrange(
+                        "g (p j) c -> p g (j c)", j=PACK
+                    ),
+                )
+            g_records = g_raw[:, :, 0:RECORD].rearrange("p g (j c) -> p g j c", j=PACK)
+
+            g_words = words_pool.tile([P, POSITIONS, G_TILE], U32, align_bytes=64)
+            g_scales = words_pool.tile([P, POSITIONS, G_TILE], U8, align_bytes=64)
+            for c0, n in power_of_two_runs(POSITIONS):
+                g_grouped = grouped_pool.tile([P, RUN, G_TILE, PACK], BF16, align_bytes=64)
+                regroup(
+                    nc,
+                    turn,
+                    out=g_grouped[:, 0:n, :, :].rearrange("p c g j -> p g j c"),
+                    in_=g_records[:, :, :, c0 : c0 + n],
+                )
+                turn += 1
+                nc.vector.quantize_mx(
+                    out=g_words[:, c0 : c0 + n, :].rearrange("p c g -> p (c g)").bitcast(E5M2_X4),
+                    scales=g_scales[:, c0 : c0 + n, :].rearrange("p c g -> p (c g)"),
+                    in_=g_grouped[:, 0:n, :, :].rearrange("p c g j -> p (c g j)"),
+                )
+
+            planes = planes_pool.tile([P, COEFFS, F_IN], F32)
+            c_l = 0
+            for l in range(DEGREES):
+                d = 2 * l + 1
+                s = l * l
+                sums = [psum.tile([P, F_IN], F32, name="sums") for m in range(d)]
+                for u in range(d):
+                    for m in range(d):
+                        c = c_l + u * d + m
+                        nc.tensor.matmul_mx(
+                            out=sums[m][:],
+                            lhsT=g_words[:, c, :].bitcast(E5M2_X4),
+                            lhsT_scale=g_scales[:, c, :],
+                            rhs=x_words[:, s + u, :].bitcast(E4M3_X4),
+                            rhs_scale=x_scales[:, s + u, :],
+                            start=(u == 0),
+                            stop=(u == d - 1),
+                        )
+                for m in range(d):
+                    nc.scalar.mul(out=planes[:, s + m, :], in_=sums[m][:], mul=SCALE)
+                c_l += d * d
+
+            for f0 in range(0, F_IN, F_HALF):
+                result = result_pool.tile([P, F_HALF, COEFFS], F32)
+                nc.vector.tensor_copy(
+                    out=result[:], in_=planes[:, :, f0 : f0 + F_HALF].rearrange("p i f -> p f i")
+                )
+                nc.scalar.dma_start(out=out[g0 : g0 + G_TILE, f0 : f0 + F_HALF, :], in_=result[:])

@@ -26,7 +26,10 @@ RUN = 4
 RECORD = PACK * POSITIONS
 RECORD_PITCH = 144
 F_PIECE = 128
-F_HALF = 256
+F_PIECES = F_IN // F_PIECE
+RAW_TILES = 2
+KEPT_TILES = 3
+LAG = 2
 
 FLOPS = 2 * BATCH * F_IN * G_OUT * POSITIONS
 BYTES = 2 * BATCH * F_IN * COEFFS + 2 * G_OUT * BATCH * POSITIONS + 4 * G_OUT * F_IN * COEFFS
@@ -81,76 +84,118 @@ def quantise_x(tc, x, x_words, x_scales):
             )
 
 
+def load_grad_tile(nc, raw_pool, grad_out, g0):
+    g_raw = raw_pool.tile([P, G_TILE, RECORD_PITCH], BF16, name="g_raw")
+    for h0 in range(0, G_TILE, G_TILE // 2):
+        nc.sync.dma_start(
+            out=g_raw[:, h0 : h0 + G_TILE // 2, 0:RECORD],
+            in_=grad_out[g0 + h0 : g0 + h0 + G_TILE // 2].rearrange("g (p j) c -> p g (j c)", j=PACK),
+        )
+    return g_raw
+
+
+def quantise_grad_tile(nc, grouped_pool, words_pool, g_raw):
+    g_records = g_raw[:, :, 0:RECORD].rearrange("p g (j c) -> p g j c", j=PACK)
+    g_words = words_pool.tile([P, POSITIONS, G_TILE], U32, align_bytes=64, name="g_words")
+    g_scales = words_pool.tile([P, POSITIONS, G_TILE], U8, align_bytes=64, name="g_scales")
+    runs = power_of_two_runs(POSITIONS)
+    grouped = {}
+    for r in range(len(runs) + LAG):
+        if r < len(runs):
+            c0, n = runs[r]
+            grouped[r] = grouped_pool.tile([P, RUN, G_TILE, PACK], BF16, align_bytes=64, name="g_grouped")
+            regroup(
+                nc,
+                r,
+                out=grouped[r][:, 0:n, :, :].rearrange("p c g j -> p g j c"),
+                in_=g_records[:, :, :, c0 : c0 + n],
+            )
+        if r >= LAG:
+            c0, n = runs[r - LAG]
+            nc.vector.quantize_mx(
+                out=g_words[:, c0 : c0 + n, :].rearrange("p c g -> p (c g)").bitcast(E5M2_X4),
+                scales=g_scales[:, c0 : c0 + n, :].rearrange("p c g -> p (c g)"),
+                in_=grouped[r - LAG][:, 0:n, :, :].rearrange("p c g j -> p (c g j)"),
+            )
+    return g_words, g_scales
+
+
+def multiply(nc, psum, planes_pool, g_words, g_scales, x_words, x_scales):
+    planes = planes_pool.tile([P, COEFFS, F_IN], F32, name="planes")
+    c_l = 0
+    for l in range(DEGREES):
+        d = 2 * l + 1
+        s = l * l
+        sums = [psum.tile([P, F_IN], F32, name="sums") for m in range(d)]
+        for u in range(d):
+            for m in range(d):
+                c = c_l + u * d + m
+                nc.tensor.matmul_mx(
+                    out=sums[m][:],
+                    lhsT=g_words[:, c, :].bitcast(E5M2_X4),
+                    lhsT_scale=g_scales[:, c, :],
+                    rhs=x_words[:, s + u, :].bitcast(E4M3_X4),
+                    rhs_scale=x_scales[:, s + u, :],
+                    start=(u == 0),
+                    stop=(u == d - 1),
+                )
+        for m in range(d):
+            if m % 2 == 0:
+                nc.scalar.mul(out=planes[:, s + m, :], in_=sums[m][:], mul=SCALE)
+            else:
+                nc.vector.tensor_scalar_mul(out=planes[:, s + m, :], in0=sums[m][:], scalar1=SCALE)
+        c_l += d * d
+    return planes
+
+
+def weave(nc, result_pool, planes):
+    pieces = []
+    for q in range(F_PIECES):
+        result = result_pool.tile([P, F_PIECE, COEFFS], F32, name="result")
+        woven = planes[:, :, q * F_PIECE : (q + 1) * F_PIECE].rearrange("p i f -> p f i")
+        if q % 3 == 1:
+            nc.scalar.copy(out=result[:], in_=woven)
+        else:
+            nc.vector.tensor_copy(out=result[:], in_=woven)
+        pieces.append(result)
+    return pieces
+
+
+def store(nc, out, g0, pieces):
+    for q in range(F_PIECES):
+        nc.sync.dma_start(
+            out=out[g0 : g0 + G_TILE, q * F_PIECE : (q + 1) * F_PIECE, :], in_=pieces[q][:]
+        )
+
+
 def tile_s2conv_pa_kernel(tc, x, psi, grad_out, out):
     nc = tc.nc
     with ExitStack() as pools:
+        pools.enter_context(tc.manual_schedule())
         keep = pools.enter_context(tc.tile_pool(name="keep", bufs=1))
-        raw_pool = pools.enter_context(tc.tile_pool(name="grad_raw", bufs=3))
+        raw_pool = pools.enter_context(tc.tile_pool(name="grad_raw", bufs=RAW_TILES))
 
         x_words = keep.tile([P, COEFFS, F_IN], U32, align_bytes=64)
         x_scales = keep.tile([P, COEFFS, F_IN], U8, align_bytes=64)
         quantise_x(tc, x, x_words, x_scales)
 
-        grouped_pool = pools.enter_context(tc.tile_pool(name="grad_grouped", bufs=4))
+        grouped_pool = pools.enter_context(tc.tile_pool(name="grad_grouped", bufs=LAG + 2))
         words_pool = pools.enter_context(tc.tile_pool(name="grad_words", bufs=2))
         planes_pool = pools.enter_context(tc.tile_pool(name="planes", bufs=1))
-        result_pool = pools.enter_context(tc.tile_pool(name="result", bufs=2))
+        result_pool = pools.enter_context(tc.tile_pool(name="result", bufs=KEPT_TILES * F_PIECES))
         psum = pools.enter_context(tc.psum_pool(name="psum", bufs=8))
 
-        turn = 0
-        for g0 in range(0, G_OUT, G_TILE):
-            g_raw = raw_pool.tile([P, G_TILE, RECORD_PITCH], BF16)
-            for h0 in range(0, G_TILE, G_TILE // 2):
-                nc.sync.dma_start(
-                    out=g_raw[:, h0 : h0 + G_TILE // 2, 0:RECORD],
-                    in_=grad_out[g0 + h0 : g0 + h0 + G_TILE // 2].rearrange(
-                        "g (p j) c -> p g (j c)", j=PACK
-                    ),
-                )
-            g_records = g_raw[:, :, 0:RECORD].rearrange("p g (j c) -> p g j c", j=PACK)
+        raw = {}
+        for t in range(RAW_TILES):
+            raw[t] = load_grad_tile(nc, raw_pool, grad_out, t * G_TILE)
 
-            g_words = words_pool.tile([P, POSITIONS, G_TILE], U32, align_bytes=64)
-            g_scales = words_pool.tile([P, POSITIONS, G_TILE], U8, align_bytes=64)
-            for c0, n in power_of_two_runs(POSITIONS):
-                g_grouped = grouped_pool.tile([P, RUN, G_TILE, PACK], BF16, align_bytes=64)
-                regroup(
-                    nc,
-                    turn,
-                    out=g_grouped[:, 0:n, :, :].rearrange("p c g j -> p g j c"),
-                    in_=g_records[:, :, :, c0 : c0 + n],
-                )
-                turn += 1
-                nc.vector.quantize_mx(
-                    out=g_words[:, c0 : c0 + n, :].rearrange("p c g -> p (c g)").bitcast(E5M2_X4),
-                    scales=g_scales[:, c0 : c0 + n, :].rearrange("p c g -> p (c g)"),
-                    in_=g_grouped[:, 0:n, :, :].rearrange("p c g j -> p (c g j)"),
-                )
-
-            planes = planes_pool.tile([P, COEFFS, F_IN], F32)
-            c_l = 0
-            for l in range(DEGREES):
-                d = 2 * l + 1
-                s = l * l
-                sums = [psum.tile([P, F_IN], F32, name="sums") for m in range(d)]
-                for u in range(d):
-                    for m in range(d):
-                        c = c_l + u * d + m
-                        nc.tensor.matmul_mx(
-                            out=sums[m][:],
-                            lhsT=g_words[:, c, :].bitcast(E5M2_X4),
-                            lhsT_scale=g_scales[:, c, :],
-                            rhs=x_words[:, s + u, :].bitcast(E4M3_X4),
-                            rhs_scale=x_scales[:, s + u, :],
-                            start=(u == 0),
-                            stop=(u == d - 1),
-                        )
-                for m in range(d):
-                    nc.scalar.mul(out=planes[:, s + m, :], in_=sums[m][:], mul=SCALE)
-                c_l += d * d
-
-            for f0 in range(0, F_IN, F_HALF):
-                result = result_pool.tile([P, F_HALF, COEFFS], F32)
-                nc.vector.tensor_copy(
-                    out=result[:], in_=planes[:, :, f0 : f0 + F_HALF].rearrange("p i f -> p f i")
-                )
-                nc.scalar.dma_start(out=out[g0 : g0 + G_TILE, f0 : f0 + F_HALF, :], in_=result[:])
+        results = {}
+        for t in range(N_G_TILES):
+            g_words, g_scales = quantise_grad_tile(nc, grouped_pool, words_pool, raw[t])
+            if t + RAW_TILES < N_G_TILES:
+                raw[t + RAW_TILES] = load_grad_tile(nc, raw_pool, grad_out, (t + RAW_TILES) * G_TILE)
+            if t >= 1:
+                store(nc, out, (t - 1) * G_TILE, results[t - 1])
+            planes = multiply(nc, psum, planes_pool, g_words, g_scales, x_words, x_scales)
+            results[t] = weave(nc, result_pool, planes)
+        store(nc, out, (N_G_TILES - 1) * G_TILE, results[N_G_TILES - 1])

@@ -2,6 +2,7 @@ import math
 from contextlib import ExitStack
 
 import concourse.mybir as mybir
+from concourse.masks import make_identity
 
 BF16 = mybir.dt.bfloat16
 F32 = mybir.dt.float32
@@ -28,8 +29,8 @@ RECORD_PITCH = 144
 F_PIECE = 128
 F_PIECES = F_IN // F_PIECE
 RAW_TILES = 2
-KEPT_TILES = 3
-LAG = 2
+LEAD = 2
+KINDS = ("rows", "records", "rows", "records")
 
 FLOPS = 2 * BATCH * F_IN * G_OUT * POSITIONS
 BYTES = 2 * BATCH * F_IN * COEFFS + 2 * G_OUT * BATCH * POSITIONS + 4 * G_OUT * F_IN * COEFFS
@@ -62,7 +63,6 @@ def quantise_x(tc, x, x_words, x_scales):
         for f0 in range(0, F_IN, F_PIECE):
             piece = slice(f0, f0 + F_PIECE)
             nc.sync.dma_start(out=x_raw[:, :, piece, :], in_=x_rows[:, :, piece, :])
-
         x_grouped = stage.tile([P, COEFFS, F_IN, PACK], BF16, align_bytes=64)
         turn = 0
         for f0 in range(0, F_IN, F_PIECE):
@@ -75,7 +75,6 @@ def quantise_x(tc, x, x_words, x_scales):
                     in_=x_raw[:, :, piece, i0 : i0 + n].rearrange("p j f i -> p f j i"),
                 )
                 turn += 1
-
         for i in range(COEFFS):
             nc.vector.quantize_mx(
                 out=x_words[:, i, :].bitcast(E4M3_X4),
@@ -84,88 +83,31 @@ def quantise_x(tc, x, x_words, x_scales):
             )
 
 
-def load_grad_tile(nc, raw_pool, grad_out, g0):
-    g_raw = raw_pool.tile([P, G_TILE, RECORD_PITCH], BF16, name="g_raw")
-    for h0 in range(0, G_TILE, G_TILE // 2):
-        nc.sync.dma_start(
-            out=g_raw[:, h0 : h0 + G_TILE // 2, 0:RECORD],
-            in_=grad_out[g0 + h0 : g0 + h0 + G_TILE // 2].rearrange("g (p j) c -> p g (j c)", j=PACK),
-        )
+def load_grad_tile(nc, raw_pool, grad_out, t):
+    g0 = t * G_TILE
+    if KINDS[t] == "records":
+        g_raw = raw_pool.tile([P, G_TILE, RECORD_PITCH], BF16, name="g_raw")
+        for h0 in range(0, G_TILE, G_TILE // 2):
+            nc.sync.dma_start(
+                out=g_raw[:, h0 : h0 + G_TILE // 2, 0:RECORD],
+                in_=grad_out[g0 + h0 : g0 + h0 + G_TILE // 2].rearrange("g (p j) c -> p g (j c)", j=PACK),
+            )
+        return g_raw[:, :, 0:RECORD].rearrange("p g (j c) -> p g j c", j=PACK)
+    g_raw = raw_pool.tile([P, P, RECORD], BF16, name="g_raw")
+    rows = grad_out[g0 : g0 + G_TILE].rearrange("g (p j) c -> g p (j c)", j=PACK)
+    for p0 in range(0, P, P // 4):
+        nc.sync.dma_start(out=g_raw[:, p0 : p0 + P // 4, :], in_=rows[:, p0 : p0 + P // 4, :])
     return g_raw
 
 
-def quantise_grad_tile(nc, grouped_pool, words_pool, g_raw):
-    g_records = g_raw[:, :, 0:RECORD].rearrange("p g (j c) -> p g j c", j=PACK)
-    g_words = words_pool.tile([P, POSITIONS, G_TILE], U32, align_bytes=64, name="g_words")
-    g_scales = words_pool.tile([P, POSITIONS, G_TILE], U8, align_bytes=64, name="g_scales")
-    runs = power_of_two_runs(POSITIONS)
-    grouped = {}
-    for r in range(len(runs) + LAG):
-        if r < len(runs):
-            c0, n = runs[r]
-            grouped[r] = grouped_pool.tile([P, RUN, G_TILE, PACK], BF16, align_bytes=64, name="g_grouped")
-            regroup(
-                nc,
-                r,
-                out=grouped[r][:, 0:n, :, :].rearrange("p c g j -> p g j c"),
-                in_=g_records[:, :, :, c0 : c0 + n],
-            )
-        if r >= LAG:
-            c0, n = runs[r - LAG]
-            nc.vector.quantize_mx(
-                out=g_words[:, c0 : c0 + n, :].rearrange("p c g -> p (c g)").bitcast(E5M2_X4),
-                scales=g_scales[:, c0 : c0 + n, :].rearrange("p c g -> p (c g)"),
-                in_=grouped[r - LAG][:, 0:n, :, :].rearrange("p c g j -> p (c g j)"),
-            )
-    return g_words, g_scales
-
-
-def multiply(nc, psum, planes_pool, g_words, g_scales, x_words, x_scales):
-    planes = planes_pool.tile([P, COEFFS, F_IN], F32, name="planes")
+def position(c):
     c_l = 0
     for l in range(DEGREES):
         d = 2 * l + 1
-        s = l * l
-        sums = [psum.tile([P, F_IN], F32, name="sums") for m in range(d)]
-        for u in range(d):
-            for m in range(d):
-                c = c_l + u * d + m
-                nc.tensor.matmul_mx(
-                    out=sums[m][:],
-                    lhsT=g_words[:, c, :].bitcast(E5M2_X4),
-                    lhsT_scale=g_scales[:, c, :],
-                    rhs=x_words[:, s + u, :].bitcast(E4M3_X4),
-                    rhs_scale=x_scales[:, s + u, :],
-                    start=(u == 0),
-                    stop=(u == d - 1),
-                )
-        for m in range(d):
-            if m % 2 == 0:
-                nc.scalar.mul(out=planes[:, s + m, :], in_=sums[m][:], mul=SCALE)
-            else:
-                nc.vector.tensor_scalar_mul(out=planes[:, s + m, :], in0=sums[m][:], scalar1=SCALE)
+        if c < c_l + d * d:
+            return l, (c - c_l) // d, (c - c_l) % d
         c_l += d * d
-    return planes
-
-
-def weave(nc, result_pool, planes):
-    pieces = []
-    for q in range(F_PIECES):
-        result = result_pool.tile([P, F_PIECE, COEFFS], F32, name="result")
-        woven = planes[:, :, q * F_PIECE : (q + 1) * F_PIECE].rearrange("p i f -> p f i")
-        if q % 3 == 1:
-            nc.scalar.copy(out=result[:], in_=woven)
-        else:
-            nc.vector.tensor_copy(out=result[:], in_=woven)
-        pieces.append(result)
-    return pieces
-
-
-def store(nc, out, g0, pieces):
-    for q in range(F_PIECES):
-        nc.sync.dma_start(
-            out=out[g0 : g0 + G_TILE, q * F_PIECE : (q + 1) * F_PIECE, :], in_=pieces[q][:]
-        )
+    raise ValueError("no such position")
 
 
 def tile_s2conv_pa_kernel(tc, x, psi, grad_out, out):
@@ -174,28 +116,120 @@ def tile_s2conv_pa_kernel(tc, x, psi, grad_out, out):
         pools.enter_context(tc.manual_schedule())
         keep = pools.enter_context(tc.tile_pool(name="keep", bufs=1))
         raw_pool = pools.enter_context(tc.tile_pool(name="grad_raw", bufs=RAW_TILES))
+        grouped_pool = pools.enter_context(tc.tile_pool(name="grad_grouped", bufs=3))
+        words_pool = pools.enter_context(tc.tile_pool(name="grad_words", bufs=3))
 
+        ident = keep.tile([P, P], BF16)
+        make_identity(nc, ident[:])
         x_words = keep.tile([P, COEFFS, F_IN], U32, align_bytes=64)
         x_scales = keep.tile([P, COEFFS, F_IN], U8, align_bytes=64)
         quantise_x(tc, x, x_words, x_scales)
 
-        grouped_pool = pools.enter_context(tc.tile_pool(name="grad_grouped", bufs=LAG + 2))
-        words_pool = pools.enter_context(tc.tile_pool(name="grad_words", bufs=2))
-        planes_pool = pools.enter_context(tc.tile_pool(name="planes", bufs=1))
-        result_pool = pools.enter_context(tc.tile_pool(name="result", bufs=KEPT_TILES * F_PIECES))
-        psum = pools.enter_context(tc.psum_pool(name="psum", bufs=8))
+        planes_pool = pools.enter_context(tc.tile_pool(name="planes", bufs=2))
+        result_pool = pools.enter_context(tc.tile_pool(name="result", bufs=2 * F_PIECES))
+        sums_pool = pools.enter_context(tc.psum_pool(name="sums", bufs=5))
+        flip_pool = pools.enter_context(tc.psum_pool(name="flip", bufs=3))
+
+        rounds = [(t, c0, min(RUN, POSITIONS - c0)) for t in range(N_G_TILES) for c0 in range(0, POSITIONS, RUN)]
+        per_tile = len(rounds) // N_G_TILES
+        n_rounds = len(rounds)
 
         raw = {}
         for t in range(RAW_TILES):
-            raw[t] = load_grad_tile(nc, raw_pool, grad_out, t * G_TILE)
+            raw[t] = load_grad_tile(nc, raw_pool, grad_out, t)
 
-        results = {}
-        for t in range(N_G_TILES):
-            g_words, g_scales = quantise_grad_tile(nc, grouped_pool, words_pool, raw[t])
-            if t + RAW_TILES < N_G_TILES:
-                raw[t + RAW_TILES] = load_grad_tile(nc, raw_pool, grad_out, (t + RAW_TILES) * G_TILE)
-            if t >= 1:
-                store(nc, out, (t - 1) * G_TILE, results[t - 1])
-            planes = multiply(nc, psum, planes_pool, g_words, g_scales, x_words, x_scales)
-            results[t] = weave(nc, result_pool, planes)
-        store(nc, out, (N_G_TILES - 1) * G_TILE, results[N_G_TILES - 1])
+        flips = {}
+        grouped = {}
+        words = {}
+        sums = {}
+        planes = {}
+        closed = []
+        weaves = []
+
+        for s in range(-LEAD, n_rounds + 1 + F_PIECES):
+            p = s + LEAD
+            if p < n_rounds and KINDS[rounds[p][0]] == "rows":
+                t, c0, n = rounds[p]
+                flips[p] = []
+                for h0 in range(0, n, 2):
+                    k = min(2, n - h0)
+                    flip = flip_pool.tile([P, 2, PACK, G_TILE], BF16, name="flip")
+                    for cc in range(k):
+                        for j in range(PACK):
+                            nc.tensor.transpose(
+                                out=flip[:, cc, j, :],
+                                in_=raw[t][:, :, j * POSITIONS + c0 + h0 + cc],
+                                identity=ident[:],
+                            )
+                    flips[p].append((h0, k, flip))
+            if 0 <= p - 1 < n_rounds:
+                t, c0, n = rounds[p - 1]
+                g_words = words_pool.tile([P, RUN, G_TILE], U32, align_bytes=64, name="g_words")
+                g_scales = words_pool.tile([P, RUN, G_TILE], U8, align_bytes=64, name="g_scales")
+                for a, k in power_of_two_runs(n):
+                    nc.vector.quantize_mx(
+                        out=g_words[:, a : a + k, :].rearrange("p c g -> p (c g)").bitcast(E5M2_X4),
+                        scales=g_scales[:, a : a + k, :].rearrange("p c g -> p (c g)"),
+                        in_=grouped[p - 1][:, a : a + k, :, :].rearrange("p c g j -> p (c g j)"),
+                    )
+                words[p - 1] = (g_words, g_scales)
+            for t, i, bank in closed:
+                if t not in planes:
+                    planes[t] = planes_pool.tile([P, COEFFS, F_IN], F32, name="planes")
+                if i % 2 == 0:
+                    nc.scalar.mul(out=planes[t][:, i, :], in_=bank[:], mul=SCALE)
+                else:
+                    nc.vector.tensor_scalar_mul(out=planes[t][:, i, :], in0=bank[:], scalar1=SCALE)
+                if i == COEFFS - 1:
+                    weaves.extend((t, q) for q in range(F_PIECES))
+            closed.clear()
+            for turn in range(len(weaves) if s >= n_rounds else min(1, len(weaves))):
+                t, q = weaves.pop(0)
+                result = result_pool.tile([P, F_PIECE, COEFFS], F32, name="result")
+                woven = planes[t][:, :, q * F_PIECE : (q + 1) * F_PIECE].rearrange("p i f -> p f i")
+                if q % 3 == 1:
+                    nc.scalar.copy(out=result[:], in_=woven)
+                else:
+                    nc.vector.tensor_copy(out=result[:], in_=woven)
+                nc.sync.dma_start(
+                    out=out[t * G_TILE : (t + 1) * G_TILE, q * F_PIECE : (q + 1) * F_PIECE, :], in_=result[:]
+                )
+            if p < n_rounds:
+                t, c0, n = rounds[p]
+                grouped[p] = grouped_pool.tile([P, RUN, G_TILE, PACK], BF16, align_bytes=64, name="g_grouped")
+                if KINDS[t] == "rows":
+                    for turn, (h0, k, flip) in enumerate(flips[p]):
+                        regroup(
+                            nc,
+                            turn,
+                            out=grouped[p][:, h0 : h0 + k, :, :],
+                            in_=flip[:, 0:k, :, :].rearrange("p c j g -> p c g j"),
+                        )
+                else:
+                    regroup(
+                        nc,
+                        p,
+                        out=grouped[p][:, 0:n, :, :].rearrange("p c g j -> p g j c"),
+                        in_=raw[t][:, :, :, c0 : c0 + n],
+                    )
+                if (p + 1) % per_tile == 0 and t + RAW_TILES < N_G_TILES:
+                    raw[t + RAW_TILES] = load_grad_tile(nc, raw_pool, grad_out, t + RAW_TILES)
+            if 0 <= s < n_rounds:
+                t, c0, n = rounds[s]
+                g_words, g_scales = words[s]
+                for cc in range(n):
+                    l, u, m = position(c0 + cc)
+                    d = 2 * l + 1
+                    if u == 0:
+                        sums[(t, l, m)] = sums_pool.tile([P, F_IN], F32, name="sums")
+                    nc.tensor.matmul_mx(
+                        out=sums[(t, l, m)][:],
+                        lhsT=g_words[:, cc, :].bitcast(E5M2_X4),
+                        lhsT_scale=g_scales[:, cc, :],
+                        rhs=x_words[:, l * l + u, :].bitcast(E4M3_X4),
+                        rhs_scale=x_scales[:, l * l + u, :],
+                        start=(u == 0),
+                        stop=(u == d - 1),
+                    )
+                    if u == d - 1:
+                        closed.append((t, l * l + m, sums[(t, l, m)]))

@@ -30,6 +30,7 @@ F_PIECE = 128
 F_PIECES = F_IN // F_PIECE
 RAW_TILES = 2
 LEAD = 2
+PAIRS = PACK // 2
 KINDS = ("rows", "records", "rows", "records")
 
 FLOPS = 2 * BATCH * F_IN * G_OUT * POSITIONS
@@ -93,10 +94,11 @@ def load_grad_tile(nc, raw_pool, grad_out, t):
                 in_=grad_out[g0 + h0 : g0 + h0 + G_TILE // 2].rearrange("g (p j) c -> p g (j c)", j=PACK),
             )
         return g_raw[:, :, 0:RECORD].rearrange("p g (j c) -> p g j c", j=PACK)
-    g_raw = raw_pool.tile([P, P, RECORD], BF16, name="g_raw")
-    rows = grad_out[g0 : g0 + G_TILE].rearrange("g (p j) c -> g p (j c)", j=PACK)
-    for p0 in range(0, P, P // 4):
-        nc.sync.dma_start(out=g_raw[:, p0 : p0 + P // 4, :], in_=rows[:, p0 : p0 + P // 4, :])
+    g_raw = raw_pool.tile([P, BATCH, POSITIONS], BF16, name="g_raw")
+    for b0 in range(0, BATCH, BATCH // 4):
+        nc.sync.dma_start(
+            out=g_raw[:, b0 : b0 + BATCH // 4, :], in_=grad_out[g0 : g0 + G_TILE, b0 : b0 + BATCH // 4, :]
+        )
     return g_raw
 
 
@@ -118,8 +120,9 @@ def tile_s2conv_pa_kernel(tc, x, psi, grad_out, out):
         raw_pool = pools.enter_context(tc.tile_pool(name="grad_raw", bufs=RAW_TILES))
         grouped_pool = pools.enter_context(tc.tile_pool(name="grad_grouped", bufs=3))
         words_pool = pools.enter_context(tc.tile_pool(name="grad_words", bufs=3))
+        straight_pool = pools.enter_context(tc.tile_pool(name="grad_straight", bufs=3))
 
-        ident = keep.tile([P, P], BF16)
+        ident = keep.tile([P, P], F32)
         make_identity(nc, ident[:])
         x_words = keep.tile([P, COEFFS, F_IN], U32, align_bytes=64)
         x_scales = keep.tile([P, COEFFS, F_IN], U8, align_bytes=64)
@@ -139,6 +142,7 @@ def tile_s2conv_pa_kernel(tc, x, psi, grad_out, out):
             raw[t] = load_grad_tile(nc, raw_pool, grad_out, t)
 
         flips = {}
+        straight = {}
         grouped = {}
         words = {}
         sums = {}
@@ -146,19 +150,20 @@ def tile_s2conv_pa_kernel(tc, x, psi, grad_out, out):
         closed = []
         weaves = []
 
-        for s in range(-LEAD, n_rounds + 1 + F_PIECES):
+        for s in range(-LEAD - 1, n_rounds + 1 + F_PIECES):
             p = s + LEAD
-            if p < n_rounds and KINDS[rounds[p][0]] == "rows":
+            if 0 <= p < n_rounds and KINDS[rounds[p][0]] == "rows":
                 t, c0, n = rounds[p]
                 flips[p] = []
                 for h0 in range(0, n, 2):
                     k = min(2, n - h0)
-                    flip = flip_pool.tile([P, 2, PACK, G_TILE], BF16, name="flip")
+                    flip = flip_pool.tile([P, 2, PAIRS, G_TILE], F32, name="flip")
                     for cc in range(k):
-                        for j in range(PACK):
+                        pairs = straight[p][:, h0 + cc, :].bitcast(F32)
+                        for u in range(PAIRS):
                             nc.tensor.transpose(
-                                out=flip[:, cc, j, :],
-                                in_=raw[t][:, :, j * POSITIONS + c0 + h0 + cc],
+                                out=flip[:, cc, u, :],
+                                in_=pairs[:, u : BATCH // 2 : PAIRS],
                                 identity=ident[:],
                             )
                     flips[p].append((h0, k, flip))
@@ -176,7 +181,7 @@ def tile_s2conv_pa_kernel(tc, x, psi, grad_out, out):
             for t, i, bank in closed:
                 if t not in planes:
                     planes[t] = planes_pool.tile([P, COEFFS, F_IN], F32, name="planes")
-                if i % 2 == 0:
+                if i % 2 == 0 or KINDS[t] == "rows":
                     nc.scalar.mul(out=planes[t][:, i, :], in_=bank[:], mul=SCALE)
                 else:
                     nc.vector.tensor_scalar_mul(out=planes[t][:, i, :], in0=bank[:], scalar1=SCALE)
@@ -194,16 +199,25 @@ def tile_s2conv_pa_kernel(tc, x, psi, grad_out, out):
                 nc.sync.dma_start(
                     out=out[t * G_TILE : (t + 1) * G_TILE, q * F_PIECE : (q + 1) * F_PIECE, :], in_=result[:]
                 )
-            if p < n_rounds:
+            if p + 1 < n_rounds and KINDS[rounds[p + 1][0]] == "rows":
+                t, c0, n = rounds[p + 1]
+                straight[p + 1] = straight_pool.tile([P, RUN, BATCH], BF16, align_bytes=64, name="g_straight")
+                nc.vector.tensor_copy(
+                    out=straight[p + 1][:, 0:n, :].rearrange("g c b -> g b c"), in_=raw[t][:, :, c0 : c0 + n]
+                )
+                if (p + 2) % per_tile == 0 and t + RAW_TILES < N_G_TILES:
+                    raw[t + RAW_TILES] = load_grad_tile(nc, raw_pool, grad_out, t + RAW_TILES)
+            if 0 <= p < n_rounds:
                 t, c0, n = rounds[p]
                 grouped[p] = grouped_pool.tile([P, RUN, G_TILE, PACK], BF16, align_bytes=64, name="g_grouped")
                 if KINDS[t] == "rows":
-                    for turn, (h0, k, flip) in enumerate(flips[p]):
-                        regroup(
-                            nc,
-                            turn,
-                            out=grouped[p][:, h0 : h0 + k, :, :],
-                            in_=flip[:, 0:k, :, :].rearrange("p c j g -> p c g j"),
+                    for h0, k, flip in flips[p]:
+                        nc.scalar.copy(
+                            out=grouped[p][:, h0 : h0 + k, :, :]
+                            .rearrange("p c g j -> p (c g j)")
+                            .bitcast(F32)
+                            .rearrange("p (c g u) -> p c g u", c=k, u=PAIRS),
+                            in_=flip[:, 0:k, :, :].rearrange("p c u g -> p c g u"),
                         )
                 else:
                     regroup(
@@ -212,7 +226,7 @@ def tile_s2conv_pa_kernel(tc, x, psi, grad_out, out):
                         out=grouped[p][:, 0:n, :, :].rearrange("p c g j -> p g j c"),
                         in_=raw[t][:, :, :, c0 : c0 + n],
                     )
-                if (p + 1) % per_tile == 0 and t + RAW_TILES < N_G_TILES:
+                if KINDS[t] == "records" and (p + 1) % per_tile == 0 and t + RAW_TILES < N_G_TILES:
                     raw[t + RAW_TILES] = load_grad_tile(nc, raw_pool, grad_out, t + RAW_TILES)
             if 0 <= s < n_rounds:
                 t, c0, n = rounds[s]

@@ -28,7 +28,7 @@ RECORD = PACK * POSITIONS
 RECORD_PITCH = 144
 F_PIECE = 128
 F_PIECES = F_IN // F_PIECE
-RAW_TILES = 2
+RAW_TILES = 3
 LEAD = 2
 PAIRS = PACK // 2
 KINDS = ("rows", "records", "rows", "records")
@@ -115,12 +115,9 @@ def position(c):
 def tile_s2conv_pa_kernel(tc, x, psi, grad_out, out):
     nc = tc.nc
     with ExitStack() as pools:
-        pools.enter_context(tc.manual_schedule())
+        pools.enter_context(tc.manual_schedule(engines={mybir.EngineType.PE, mybir.EngineType.SP}))
         keep = pools.enter_context(tc.tile_pool(name="keep", bufs=1))
         raw_pool = pools.enter_context(tc.tile_pool(name="grad_raw", bufs=RAW_TILES))
-        grouped_pool = pools.enter_context(tc.tile_pool(name="grad_grouped", bufs=3))
-        words_pool = pools.enter_context(tc.tile_pool(name="grad_words", bufs=3))
-        straight_pool = pools.enter_context(tc.tile_pool(name="grad_straight", bufs=3))
 
         ident = keep.tile([P, P], F32)
         make_identity(nc, ident[:])
@@ -128,8 +125,11 @@ def tile_s2conv_pa_kernel(tc, x, psi, grad_out, out):
         x_scales = keep.tile([P, COEFFS, F_IN], U8, align_bytes=64)
         quantise_x(tc, x, x_words, x_scales)
 
+        grouped_pool = pools.enter_context(tc.tile_pool(name="grad_grouped", bufs=3))
+        words_pool = pools.enter_context(tc.tile_pool(name="grad_words", bufs=3))
+        straight_pool = pools.enter_context(tc.tile_pool(name="grad_straight", bufs=3))
         planes_pool = pools.enter_context(tc.tile_pool(name="planes", bufs=2))
-        result_pool = pools.enter_context(tc.tile_pool(name="result", bufs=2 * F_PIECES))
+        result_pool = pools.enter_context(tc.tile_pool(name="result", bufs=6))
         sums_pool = pools.enter_context(tc.psum_pool(name="sums", bufs=5))
         flip_pool = pools.enter_context(tc.psum_pool(name="flip", bufs=3))
 
@@ -199,14 +199,14 @@ def tile_s2conv_pa_kernel(tc, x, psi, grad_out, out):
                 nc.sync.dma_start(
                     out=out[t * G_TILE : (t + 1) * G_TILE, q * F_PIECE : (q + 1) * F_PIECE, :], in_=result[:]
                 )
+                if q == F_PIECES - 1 and t + RAW_TILES < N_G_TILES:
+                    raw[t + RAW_TILES] = load_grad_tile(nc, raw_pool, grad_out, t + RAW_TILES)
             if p + 1 < n_rounds and KINDS[rounds[p + 1][0]] == "rows":
                 t, c0, n = rounds[p + 1]
                 straight[p + 1] = straight_pool.tile([P, RUN, BATCH], BF16, align_bytes=64, name="g_straight")
                 nc.vector.tensor_copy(
                     out=straight[p + 1][:, 0:n, :].rearrange("g c b -> g b c"), in_=raw[t][:, :, c0 : c0 + n]
                 )
-                if (p + 2) % per_tile == 0 and t + RAW_TILES < N_G_TILES:
-                    raw[t + RAW_TILES] = load_grad_tile(nc, raw_pool, grad_out, t + RAW_TILES)
             if 0 <= p < n_rounds:
                 t, c0, n = rounds[p]
                 grouped[p] = grouped_pool.tile([P, RUN, G_TILE, PACK], BF16, align_bytes=64, name="g_grouped")
@@ -226,8 +226,6 @@ def tile_s2conv_pa_kernel(tc, x, psi, grad_out, out):
                         out=grouped[p][:, 0:n, :, :].rearrange("p c g j -> p g j c"),
                         in_=raw[t][:, :, :, c0 : c0 + n],
                     )
-                if KINDS[t] == "records" and (p + 1) % per_tile == 0 and t + RAW_TILES < N_G_TILES:
-                    raw[t + RAW_TILES] = load_grad_tile(nc, raw_pool, grad_out, t + RAW_TILES)
             if 0 <= s < n_rounds:
                 t, c0, n = rounds[s]
                 g_words, g_scales = words[s]

@@ -31,7 +31,7 @@ F_PIECES = F_IN // F_PIECE
 RAW_TILES = 3
 LEAD = 2
 PAIRS = PACK // 2
-KINDS = ("rows", "records", "rows", "records")
+KINDS = ("rows", "rows", "records", "records")
 
 FLOPS = 2 * BATCH * F_IN * G_OUT * POSITIONS
 BYTES = 2 * BATCH * F_IN * COEFFS + 2 * G_OUT * BATCH * POSITIONS + 4 * G_OUT * F_IN * COEFFS
@@ -181,10 +181,10 @@ def tile_s2conv_pa_kernel(tc, x, psi, grad_out, out):
             for t, i, bank in closed:
                 if t not in planes:
                     planes[t] = planes_pool.tile([P, COEFFS, F_IN], F32, name="planes")
-                if i % 2 == 0 or KINDS[t] == "rows":
-                    nc.scalar.mul(out=planes[t][:, i, :], in_=bank[:], mul=SCALE)
-                else:
+                if i >= 4 and i % 2 == 1:
                     nc.vector.tensor_scalar_mul(out=planes[t][:, i, :], in0=bank[:], scalar1=SCALE)
+                else:
+                    nc.scalar.mul(out=planes[t][:, i, :], in_=bank[:], mul=SCALE)
                 if i == COEFFS - 1:
                     weaves.extend((t, q) for q in range(F_PIECES))
             closed.clear()

@@ -159,11 +159,10 @@ def tile_s2conv_pa_kernel(tc, x, psi, grad_out, out):
                     k = min(2, n - h0)
                     flip = flip_pool.tile([P, 2, PAIRS, G_TILE], F32, name="flip")
                     for cc in range(k):
-                        pairs = straight[p][:, h0 + cc, :].bitcast(F32)
                         for u in range(PAIRS):
                             nc.tensor.transpose(
                                 out=flip[:, cc, u, :],
-                                in_=pairs[:, u : BATCH // 2 : PAIRS],
+                                in_=straight[p][:, h0 + cc, u, :, :].rearrange("g p e -> g (p e)").bitcast(F32),
                                 identity=ident[:],
                             )
                     flips[p].append((h0, k, flip))
@@ -203,10 +202,13 @@ def tile_s2conv_pa_kernel(tc, x, psi, grad_out, out):
                     raw[t + RAW_TILES] = load_grad_tile(nc, raw_pool, grad_out, t + RAW_TILES)
             if p + 1 < n_rounds and KINDS[rounds[p + 1][0]] == "rows":
                 t, c0, n = rounds[p + 1]
-                straight[p + 1] = straight_pool.tile([P, RUN, BATCH], BF16, align_bytes=64, name="g_straight")
-                nc.vector.tensor_copy(
-                    out=straight[p + 1][:, 0:n, :].rearrange("g c b -> g b c"), in_=raw[t][:, :, c0 : c0 + n]
-                )
+                straight[p + 1] = straight_pool.tile([P, RUN, PAIRS, P, 2], BF16, align_bytes=64, name="g_straight")
+                quads = raw[t][:].rearrange("g (p u e) c -> g p u e c", u=PAIRS, e=2)
+                for u in range(PAIRS):
+                    nc.vector.tensor_copy(
+                        out=straight[p + 1][:, 0:n, u, :, :].rearrange("g c p e -> g p e c"),
+                        in_=quads[:, :, u, :, c0 : c0 + n],
+                    )
             if 0 <= p < n_rounds:
                 t, c0, n = rounds[p]
                 grouped[p] = grouped_pool.tile([P, RUN, G_TILE, PACK], BF16, align_bytes=64, name="g_grouped")

import math
from contextlib import ExitStack

import concourse.mybir as mybir
from concourse.masks import make_identity

BF16 = mybir.dt.bfloat16
F32 = mybir.dt.float32
U32 = mybir.dt.uint32
U8 = mybir.dt.uint8
E4M3_X4 = mybir.dt.float8_e4m3fn_x4
E5M2_X4 = mybir.dt.float8_e5m2_x4

P = 128
PACK = 4
BATCH = P * PACK
F_IN = 512
G_OUT = 512
DEGREES = 3
COEFFS = DEGREES * DEGREES
POSITIONS = sum((2 * l + 1) ** 2 for l in range(DEGREES))
G_TILE = P
N_G_TILES = G_OUT // G_TILE
SCALE = 1.0 / math.sqrt(F_IN)

RUN = 4
RECORD = PACK * POSITIONS
RECORD_PITCH = 144
F_PIECE = 128
F_PIECES = F_IN // F_PIECE
RAW_TILES = 3
LEAD = 2
PAIRS = PACK // 2
KINDS = ("rows", "rows", "records", "records")

FLOPS = 2 * BATCH * F_IN * G_OUT * POSITIONS
BYTES = 2 * BATCH * F_IN * COEFFS + 2 * G_OUT * BATCH * POSITIONS + 4 * G_OUT * F_IN * COEFFS


def power_of_two_runs(total):
    runs = []
    start = 0
    length = RUN
    while start < total:
        while start + length > total:
            length //= 2
        runs.append((start, length))
        start += length
    return runs


def regroup(nc, turn, out, in_):
    if turn % 2 == 0:
        nc.vector.tensor_copy(out=out, in_=in_)
    else:
        nc.scalar.copy(out=out, in_=in_)


def quantise_x(tc, x, x_words, x_scales):
    nc = tc.nc
    with tc.tile_pool(name="x_stage", bufs=1) as stage:
        x_raw = stage.tile([P, PACK, F_IN, COEFFS], BF16)
        x_rows = x.rearrange("(p j) f i -> p j f i", j=PACK)
        for f0 in range(0, F_IN, F_PIECE):
            piece = slice(f0, f0 + F_PIECE)
            nc.sync.dma_start(out=x_raw[:, :, piece, :], in_=x_rows[:, :, piece, :])
        x_grouped = stage.tile([P, COEFFS, F_IN, PACK], BF16, align_bytes=64)
        turn = 0
        for f0 in range(0, F_IN, F_PIECE):
            piece = slice(f0, f0 + F_PIECE)
            for i0, n in power_of_two_runs(COEFFS):
                regroup(
                    nc,
                    turn,
                    out=x_grouped[:, i0 : i0 + n, piece, :].rearrange("p i f j -> p f j i"),
                    in_=x_raw[:, :, piece, i0 : i0 + n].rearrange("p j f i -> p f j i"),
                )
                turn += 1
        for i in range(COEFFS):
            nc.vector.quantize_mx(
                out=x_words[:, i, :].bitcast(E4M3_X4),
                scales=x_scales[:, i, :],
                in_=x_grouped[:, i, :, :].rearrange("p f j -> p (f j)"),
            )


def load_grad_tile(nc, raw_pool, grad_out, t):
    g0 = t * G_TILE
    if KINDS[t] == "records":
        g_raw = raw_pool.tile([P, G_TILE, RECORD_PITCH], BF16, name="g_raw")
        for h0 in range(0, G_TILE, G_TILE // 2):
            nc.sync.dma_start(
                out=g_raw[:, h0 : h0 + G_TILE // 2, 0:RECORD],
                in_=grad_out[g0 + h0 : g0 + h0 + G_TILE // 2].rearrange("g (p j) c -> p g (j c)", j=PACK),
            )
        return g_raw[:, :, 0:RECORD].rearrange("p g (j c) -> p g j c", j=PACK)
    g_raw = raw_pool.tile([P, BATCH, POSITIONS], BF16, name="g_raw")
    for b0 in range(0, BATCH, BATCH // 4):
        nc.sync.dma_start(
            out=g_raw[:, b0 : b0 + BATCH // 4, :], in_=grad_out[g0 : g0 + G_TILE, b0 : b0 + BATCH // 4, :]
        )
    return g_raw


def position(c):
    c_l = 0
    for l in range(DEGREES):
        d = 2 * l + 1
        if c < c_l + d * d:
            return l, (c - c_l) // d, (c - c_l) % d
        c_l += d * d
    raise ValueError("no such position")


def tile_s2conv_pa_kernel(tc, x, psi, grad_out, out):
    nc = tc.nc
    with ExitStack() as pools:
        pools.enter_context(tc.manual_schedule(engines={mybir.EngineType.PE, mybir.EngineType.SP}))
        keep = pools.enter_context(tc.tile_pool(name="keep", bufs=1))
        raw_pool = pools.enter_context(tc.tile_pool(name="grad_raw", bufs=RAW_TILES))

        ident = keep.tile([P, P], F32)
        make_identity(nc, ident[:])
        x_words = keep.tile([P, COEFFS, F_IN], U32, align_bytes=64)
        x_scales = keep.tile([P, COEFFS, F_IN], U8, align_bytes=64)
        quantise_x(tc, x, x_words, x_scales)

        grouped_pool = pools.enter_context(tc.tile_pool(name="grad_grouped", bufs=3))
        words_pool = pools.enter_context(tc.tile_pool(name="grad_words", bufs=3))
        straight_pool = pools.enter_context(tc.tile_pool(name="grad_straight", bufs=3))
        planes_pool = pools.enter_context(tc.tile_pool(name="planes", bufs=2))
        result_pool = pools.enter_context(tc.tile_pool(name="result", bufs=6))
        sums_pool = pools.enter_context(tc.psum_pool(name="sums", bufs=5))
        flip_pool = pools.enter_context(tc.psum_pool(name="flip", bufs=3))

        rounds = [(t, c0, min(RUN, POSITIONS - c0)) for t in range(N_G_TILES) for c0 in range(0, POSITIONS, RUN)]
        per_tile = len(rounds) // N_G_TILES
        n_rounds = len(rounds)

        raw = {}
        for t in range(RAW_TILES):
            raw[t] = load_grad_tile(nc, raw_pool, grad_out, t)

        flips = {}
        straight = {}
        grouped = {}
        words = {}
        sums = {}
        planes = {}
        closed = []
        weaves = []

        for s in range(-LEAD - 1, n_rounds + 1 + F_PIECES):
            p = s + LEAD
            if 0 <= p < n_rounds and KINDS[rounds[p][0]] == "rows":
                t, c0, n = rounds[p]
                flips[p] = []
                for h0 in range(0, n, 2):
                    k = min(2, n - h0)
                    flip = flip_pool.tile([P, 2, PAIRS, G_TILE], F32, name="flip")
                    for cc in range(k):
                        for u in range(PAIRS):
                            nc.tensor.transpose(
                                out=flip[:, cc, u, :],
                                in_=straight[p][:, h0 + cc, u, :, :].rearrange("g p e -> g (p e)").bitcast(F32),
                                identity=ident[:],
                            )
                    flips[p].append((h0, k, flip))
            if 0 <= p - 1 < n_rounds:
                t, c0, n = rounds[p - 1]
                g_words = words_pool.tile([P, RUN, G_TILE], U32, align_bytes=64, name="g_words")
                g_scales = words_pool.tile([P, RUN, G_TILE], U8, align_bytes=64, name="g_scales")
                for a, k in power_of_two_runs(n):
                    nc.vector.quantize_mx(
                        out=g_words[:, a : a + k, :].rearrange("p c g -> p (c g)").bitcast(E5M2_X4),
                        scales=g_scales[:, a : a + k, :].rearrange("p c g -> p (c g)"),
                        in_=grouped[p - 1][:, a : a + k, :, :].rearrange("p c g j -> p (c g j)"),
                    )
                words[p - 1] = (g_words, g_scales)
            for t, i, bank in closed:
                if t not in planes:
                    planes[t] = planes_pool.tile([P, COEFFS, F_IN], F32, name="planes")
                if i >= 4 and i % 2 == 1:
                    nc.vector.tensor_scalar_mul(out=planes[t][:, i, :], in0=bank[:], scalar1=SCALE)
                else:
                    nc.scalar.mul(out=planes[t][:, i, :], in_=bank[:], mul=SCALE)
                if i == COEFFS - 1:
                    weaves.extend((t, q) for q in range(F_PIECES))
            closed.clear()
            for turn in range(len(weaves) if s >= n_rounds else min(1, len(weaves))):
                t, q = weaves.pop(0)
                result = result_pool.tile([P, F_PIECE, COEFFS], F32, name="result")
                woven = planes[t][:, :, q * F_PIECE : (q + 1) * F_PIECE].rearrange("p i f -> p f i")
                if q % 3 == 1:
                    nc.scalar.copy(out=result[:], in_=woven)
                else:
                    nc.vector.tensor_copy(out=result[:], in_=woven)
                nc.sync.dma_start(
                    out=out[t * G_TILE : (t + 1) * G_TILE, q * F_PIECE : (q + 1) * F_PIECE, :], in_=result[:]
                )
                if q == F_PIECES - 1 and t + RAW_TILES < N_G_TILES:
                    raw[t + RAW_TILES] = load_grad_tile(nc, raw_pool, grad_out, t + RAW_TILES)
            if p + 1 < n_rounds and KINDS[rounds[p + 1][0]] == "rows":
                t, c0, n = rounds[p + 1]
                straight[p + 1] = straight_pool.tile([P, RUN, PAIRS, P, 2], BF16, align_bytes=64, name="g_straight")
                quads = raw[t][:].rearrange("g (p u e) c -> g p u e c", u=PAIRS, e=2)
                for u in range(PAIRS):
                    nc.vector.tensor_copy(
                        out=straight[p + 1][:, 0:n, u, :, :].rearrange("g c p e -> g p e c"),
                        in_=quads[:, :, u, :, c0 : c0 + n],
                    )
            if 0 <= p < n_rounds:
                t, c0, n = rounds[p]
                grouped[p] = grouped_pool.tile([P, RUN, G_TILE, PACK], BF16, align_bytes=64, name="g_grouped")
                if KINDS[t] == "rows":
                    for h0, k, flip in flips[p]:
                        nc.scalar.copy(
                            out=grouped[p][:, h0 : h0 + k, :, :]
                            .rearrange("p c g j -> p (c g j)")
                            .bitcast(F32)
                            .rearrange("p (c g u) -> p c g u", c=k, u=PAIRS),
                            in_=flip[:, 0:k, :, :].rearrange("p c u g -> p c g u"),
                        )
                else:
                    regroup(
                        nc,
                        p,
                        out=grouped[p][:, 0:n, :, :].rearrange("p c g j -> p g j c"),
                        in_=raw[t][:, :, :, c0 : c0 + n],
                    )
            if 0 <= s < n_rounds:
                t, c0, n = rounds[s]
                g_words, g_scales = words[s]
                for cc in range(n):
                    l, u, m = position(c0 + cc)
                    d = 2 * l + 1
                    if u == 0:
                        sums[(t, l, m)] = sums_pool.tile([P, F_IN], F32, name="sums")
                    nc.tensor.matmul_mx(
                        out=sums[(t, l, m)][:],
                        lhsT=g_words[:, cc, :].bitcast(E5M2_X4),
                        lhsT_scale=g_scales[:, cc, :],
                        rhs=x_words[:, l * l + u, :].bitcast(E4M3_X4),
                        rhs_scale=x_scales[:, l * l + u, :],
                        start=(u == 0),
                        stop=(u == d - 1),
                    )
                    if u == d - 1:
                        closed.append((t, l * l + m, sums[(t, l, m)]))
